import numpy as np
import ml_dtypes


def mxq(x, axis, fmt="e4m3"):
    dtype, down = {"e4m3": (ml_dtypes.float8_e4m3fn, 7), "e5m2": (ml_dtypes.float8_e5m2, 14)}[fmt]
    v = np.moveaxis(np.asarray(x, np.float32).astype(ml_dtypes.bfloat16).astype(np.float64), axis, -1)
    blocks = v.reshape(v.shape[:-1] + (-1, 32))
    amax = np.abs(blocks).max(-1, keepdims=True)
    byte = np.maximum(np.where(amax > 0, np.frexp(amax)[1] - 1 + 127, 0) - down, 1)
    scale = np.exp2(byte - 127.0)
    codes = (blocks / scale).astype(np.float32).astype(dtype).astype(np.float64)
    return np.moveaxis((codes * scale).reshape(v.shape), -1, axis)


WIDE = False


def mx_kscale(k):
    if not WIDE:
        return np.ones(k)
    levels = np.array([10, -10, 5, -5, 0])
    a = np.random.permutation(np.resize(levels, k // 512 * 4)).reshape(k // 512, 4)
    idx = np.arange(k)
    return np.exp2(a[idx // 512, idx % 128 // 32])


BF16 = ml_dtypes.bfloat16


def bf(x):
    return np.asarray(x, np.float32).astype(BF16)


def f64(x):
    return np.asarray(x).astype(np.float64)


B, C, H, W, P, DIM = 16, 8, 256, 256, 16, 512
SHIFT = P // 2
WD = 5 * C * P * P // 4
N = (H // P) * (W // P)
EPS = 1e-5
XS = 0.015


def patch_shift(x, shift):
    xp = np.pad(x, ((0, 0), (0, 0), (shift, shift), (shift, shift)))
    s2 = 2 * shift
    return np.concatenate([x, xp[:, :, :-s2, :-s2], xp[:, :, :-s2, s2:], xp[:, :, s2:, :-s2], xp[:, :, s2:, s2:]], axis=1)


def haar_detail_mean(x):
    b_, c_, h, w = x.shape
    r = x.reshape(b_, c_, h // 2, 2, w // 2, 2)
    return (3.0 * r[:, :, :, 0, :, 0] - r[:, :, :, 0, :, 1] - r[:, :, :, 1, :, 0] - r[:, :, :, 1, :, 1]) / 6.0


def patchify(x, p):
    b_, c_, hh, ww = x.shape
    h, w = hh // p, ww // p
    return x.reshape(b_, c_, h, p, w, p).transpose(0, 2, 4, 3, 5, 1).reshape(b_, h * w, p * p * c_)


def layernorm(u, g, b):
    m = u.mean(-1, keepdims=True)
    v = np.square(u - m).mean(-1, keepdims=True)
    return (u - m) / np.sqrt(v + EPS) * g + b


def setup_inputs():
    s = mx_kscale(WD)
    return {"x": bf(np.random.standard_normal((B, C, H, W)) * XS),
            "ln2_g": bf((1.0 + 0.1 * np.random.standard_normal(WD)) * s),
            "ln2_b": bf(0.1 * np.random.standard_normal(WD) * s),
            "w2": bf(np.random.standard_normal((WD, DIM)) / np.sqrt(WD) / s[:, None]),
            "b2": bf(0.3 * np.random.standard_normal(DIM)),
            "tok": bf(np.random.standard_normal((B, N, DIM)))}


def reference(x, ln2_g, ln2_b, w2, b2, tok):
    waves = haar_detail_mean(patch_shift(f64(x), SHIFT))
    z = layernorm(patchify(waves, P // 2), f64(ln2_g), f64(ln2_b))
    wtok = (mxq(z, 2, "e4m3") @ mxq(f64(w2), 0, "e4m3")) + f64(b2)
    return f64(tok) + wtok

@@ -1,0 +1,245 @@
+from contextlib import ExitStack
+
+import concourse.bass as bass
+import concourse.mybir as mybir
+import concourse.tile as tile
+from concourse.masks import make_identity
+
+F32 = mybir.dt.float32
+BF16 = mybir.dt.bfloat16
+U32 = mybir.dt.uint32
+U8 = mybir.dt.uint8
+FP8X4 = mybir.dt.float8_e4m3fn_x4
+ALU = mybir.AluOpType
+ACT = mybir.ActivationFunctionType
+
+P = 128
+KDIM = 2560
+DIM = 512
+FLOPS = 2 * 4096 * KDIM * DIM
+
+ROW0 = (4, 0, 0, 8, 8)
+COL0 = (4, 0, 8, 0, 8)
+V_SHIFTS = ((0, 1, 2, 3), (0, 1, 2))
+
+
+def tile_shiftedpatchtokenization_pb_t_kernel(tc, x, ln2_g, ln2_b, w2, b2, tok, out):
+    nc = tc.nc
+    xv = x.rearrange("b c (g q r) w -> g q b c (r w)", g=8, q=4)
+    wv = w2.rearrange("(g t p) n -> g p t n", t=4, p=P)
+    tok_v = tok.rearrange("b (g e j) d -> (b g) e j d", g=8, e=2)
+    out_v = out.rearrange("b (g e j) d -> (b g) e j d", g=8, e=2)
+
+    with ExitStack() as ctx:
+        keep = ctx.enter_context(tc.tile_pool(name="keep", bufs=1))
+        ident = keep.tile([P, P], F32)
+        sh_dn = keep.tile([P, P], F32)
+        sh_up = keep.tile([P, P], F32)
+        gb = keep.tile([P, P], F32)
+        b2bc = keep.tile([P, DIM], BF16)
+        wc = keep.tile([P, 5, DIM], U32, align_bytes=64)
+        ws = keep.tile([P, 5, DIM], U8, align_bytes=64)
+        W = keep.tile([P, 24, 136, 8], F32)
+        CS = keep.tile([P, 2, 4, 32], F32)
+        CR = keep.tile([P, 2, 6, 34], F32)
+        A1 = keep.tile([P, 2, 5, 34], F32)
+        Rw = keep.tile([P, 2, 2, 34], F32)
+        Bw = keep.tile([P, 2, 2, 33], F32)
+        Bc = keep.tile([P, 2, 2, 33], F32)
+        ST = keep.tile([P, 2, 2, 16], F32)
+        mean = keep.tile([P, 32], F32)
+        va = keep.tile([P, 32], F32)
+        tmp = keep.tile([P, 32], F32)
+        rstd = keep.tile([P, 32], F32)
+        nbias = keep.tile([P, 32], F32)
+        one = keep.tile([P, 1], F32)
+
+        nc.vector.memset(one[:], 1.0)
+        nc.scalar.sqrt(one[:], one[:])
+
+        make_identity(nc, ident[:])
+        nc.vector.memset(sh_dn[:], 0.0)
+        nc.vector.memset(sh_up[:], 0.0)
+        nc.vector.tensor_copy(out=sh_dn[:, 1:P], in_=ident[:, 0 : P - 1])
+        nc.vector.tensor_copy(out=sh_up[:, 0 : P - 1], in_=ident[:, 1:P])
+        nc.vector.memset(sh_dn[:].rearrange("p (a b) -> p a b", b=8)[:, :, 0:1], 0.0)
+        nc.vector.memset(sh_up[:].rearrange("p (a b) -> p a b", b=8)[:, :, 7:8], 0.0)
+        nc.vector.memset(W[:, :, 0:4, :], 0.0)
+        nc.vector.memset(W[:, :, 132:136, :], 0.0)
+        nc.vector.memset(CR[:], 0.0)
+
+        with ExitStack() as pa:
+            xpool = pa.enter_context(tc.tile_pool(name="xpool", bufs=2))
+            tpool = pa.enter_context(tc.tile_pool(name="tpool", bufs=1))
+            wpool = pa.enter_context(tc.tile_pool(name="wpool", bufs=2))
+            psa = pa.enter_context(tc.psum_pool(name="psa", bufs=2))
+
+            junk = tpool.tile([P, 4, 4, 8], F32)
+
+            def load_chunk(q):
+                xs = xpool.tile([P, 8, 2048], BF16, name="xs")
+                for g in (0, 4, 1, 5, 2, 6, 3, 7):
+                    nc.sync.dma_start(out=xs[g:P:8, :, :], in_=xv[g, q])
+                return xs
+
+            xs_next = load_chunk(0)
+
+            g0b = tpool.tile([P, P], BF16)
+            g0f = tpool.tile([P, P], F32)
+            nc.vector.memset(g0b[:], 0.0)
+            nc.sync.dma_start(out=g0b[0:20, :], in_=ln2_g.rearrange("(s p) -> s p", p=P))
+            nc.sync.dma_start(out=g0b[32:52, :], in_=ln2_b.rearrange("(s p) -> s p", p=P))
+            nc.sync.dma_start(out=b2bc[:], in_=b2.partition_broadcast(P))
+            nc.vector.tensor_copy(out=g0f[:], in_=g0b[:])
+            gps = psa.tile([P, P], F32, name="gps")
+            nc.tensor.transpose(gps[:], g0f[:], ident[:])
+            nc.vector.tensor_copy(out=gb[:], in_=gps[:])
+
+            for q in range(4):
+                xs = xs_next
+                if q < 3:
+                    xs_next = load_chunk(q + 1)
+                if q == 0:
+                    for g5 in range(5):
+                        wraw = wpool.tile([P, 4, DIM], BF16, name="wraw")
+                        nc.sync.dma_start(out=wraw[:], in_=wv[g5])
+                        wgrp = wpool.tile([P, DIM, 4], BF16, name="wgrp", align_bytes=64)
+                        nc.scalar.copy(out=wgrp[:], in_=wraw[:].rearrange("p t n -> p n t"))
+                        nc.vector.quantize_mx(
+                            out=wc[:, g5, :].bitcast(FP8X4),
+                            scales=ws[:, g5, :],
+                            in_=wgrp[:].rearrange("p n t -> p (n t)"),
+                        )
+                xq = xs[:].rearrange("p c (y e x f) -> p c y e x f", y=4, e=2, x=128, f=2)
+                t = tpool.tile([P, 8, 4, 128], F32, name="t")
+                nc.vector.scalar_tensor_tensor(
+                    out=t[:], in0=xq[:, :, :, 0, :, 0], scalar=3.0, in1=xq[:, :, :, 0, :, 1],
+                    op0=ALU.mult, op1=ALU.subtract,
+                )
+                nc.vector.tensor_tensor(out=t[:], in0=t[:], in1=xq[:, :, :, 1, :, 0], op=ALU.subtract)
+                r0 = 4 + 4 * q
+                nc.vector.tensor_tensor(
+                    out=W[:, r0 : r0 + 4, 4:132, :],
+                    in0=t[:].rearrange("p c y x -> p y x c"),
+                    in1=xq[:, :, :, 1, :, 1].rearrange("p c y x -> p y x c"),
+                    op=ALU.subtract,
+                )
+                for cx in range(32):
+                    cell = W[:, r0 : r0 + 4, 4 + 4 * cx : 8 + 4 * cx, :]
+                    nc.scalar.activation(out=junk[:], in_=cell, func=ACT.Identity, accum_out=CS[:, 0, q, cx : cx + 1])
+                    nc.scalar.activation(out=junk[:], in_=cell, func=ACT.Square, accum_out=CS[:, 1, q, cx : cx + 1])
+                if q == 0 or q == 3:
+                    sh = sh_up if q == 0 else sh_dn
+                    dst0 = 20 if q == 0 else 0
+                    for y in range(4):
+                        for h in range(2):
+                            hp = psa.tile([P, 512], F32, name="hp")
+                            cols = slice(4 + 64 * h, 68 + 64 * h)
+                            nc.tensor.matmul(
+                                out=hp[:], lhsT=sh[:], rhs=W[:, r0 + y, cols, :].rearrange("p x c -> p (x c)"),
+                                start=True, stop=True,
+                            )
+                            nc.vector.tensor_copy(out=W[:, dst0 + y, cols, :].rearrange("p x c -> p (x c)"), in_=hp[:])
+
+            cs_flat = CS[:].rearrange("p k q x -> p (k q x)")
+            pdn = psa.tile([P, 2, 4, 32], F32, name="pdn")
+            pup = psa.tile([P, 2, 4, 32], F32, name="pup")
+            nc.tensor.matmul(out=pdn[:].rearrange("p k q x -> p (k q x)"), lhsT=sh_dn[:], rhs=cs_flat, start=True, stop=True)
+            nc.tensor.matmul(out=pup[:].rearrange("p k q x -> p (k q x)"), lhsT=sh_up[:], rhs=cs_flat, start=True, stop=True)
+            nc.vector.tensor_copy(out=CR[:, :, 1:5, 1:33], in_=CS[:])
+            nc.vector.tensor_copy(out=CR[:, :, 0, 1:33], in_=pdn[:, :, 3, :])
+            nc.vector.tensor_copy(out=CR[:, :, 5, 1:33], in_=pup[:, :, 0, :])
+            nc.vector.tensor_tensor(out=A1[:], in0=CR[:, :, 0:5, :], in1=CR[:, :, 1:6, :], op=ALU.add)
+            nc.vector.tensor_tensor(out=Rw[:], in0=A1[:, :, 0:3:2, :], in1=A1[:, :, 2:5:2, :], op=ALU.add)
+            nc.vector.tensor_tensor(out=Bw[:], in0=Rw[:, :, :, 0:33], in1=Rw[:, :, :, 1:34], op=ALU.add)
+            nc.vector.tensor_tensor(out=Bc[:], in0=A1[:, :, 1:4:2, 0:33], in1=A1[:, :, 1:4:2, 1:34], op=ALU.add)
+            nc.vector.tensor_tensor(out=ST[:], in0=Bw[:, :, :, 0:31:2], in1=Bw[:, :, :, 2:33:2], op=ALU.add)
+            nc.vector.tensor_tensor(out=ST[:], in0=ST[:], in1=Bc[:, :, :, 1:32:2], op=ALU.add)
+            s1 = ST[:, 0, :, :].rearrange("p e j -> p (e j)")
+            s2 = ST[:, 1, :, :].rearrange("p e j -> p (e j)")
+            nc.vector.tensor_scalar(out=mean[:], in0=s1, scalar1=1.0 / KDIM, scalar2=None, op0=ALU.mult)
+            nc.vector.tensor_tensor(out=tmp[:], in0=mean[:], in1=mean[:], op=ALU.mult)
+            nc.vector.tensor_scalar(out=va[:], in0=s2, scalar1=1.0 / KDIM, scalar2=36.0e-5, op0=ALU.mult, op1=ALU.add)
+            nc.vector.tensor_tensor(out=va[:], in0=va[:], in1=tmp[:], op=ALU.subtract)
+            nc.scalar.sqrt(tmp[:], va[:])
+            nc.vector.reciprocal(rstd[:], tmp[:])
+            nc.vector.tensor_tensor(out=tmp[:], in0=rstd[:], in1=rstd[:], op=ALU.mult)
+            nc.vector.tensor_tensor(out=tmp[:], in0=tmp[:], in1=va[:], op=ALU.mult)
+            nc.vector.tensor_scalar(out=tmp[:], in0=tmp[:], scalar1=-0.5, scalar2=1.5, op0=ALU.mult, op1=ALU.add)
+            nc.vector.tensor_tensor(out=rstd[:], in0=rstd[:], in1=tmp[:], op=ALU.mult)
+            nc.vector.scalar_tensor_tensor(
+                out=nbias[:], in0=mean[:], scalar=-1.0, in1=rstd[:], op0=ALU.mult, op1=ALU.mult
+            )
+
+        with ExitStack() as pb:
+            npool = pb.enter_context(tc.tile_pool(name="npool", bufs=5))
+            zpool = pb.enter_context(tc.tile_pool(name="zpool", bufs=3))
+            cpool = pb.enter_context(tc.tile_pool(name="cpool", bufs=2))
+            iopool = pb.enter_context(tc.tile_pool(name="iopool", bufs=3))
+            pst = pb.enter_context(tc.psum_pool(name="pst", bufs=5))
+            psm = pb.enter_context(tc.psum_pool(name="psm", bufs=2))
+
+            for j in range(16):
+                tk = iopool.tile([P, 2, DIM], BF16, name="tk")
+                nc.sync.dma_start(out=tk[:], in_=tok_v[:, :, j, :])
+                tb = iopool.tile([P, 2, DIM], F32, name="tb")
+                for e in range(2):
+                    nc.gpsimd.tensor_tensor(out=tb[:, e, :], in0=tk[:, e, :], in1=b2bc[:], op=ALU.add)
+                nbs = []
+                for e in range(2):
+                    nb = npool.tile([P, KDIM], F32, name="nb")
+                    nbv = nb[:].rearrange("p (a b s c) -> p a b s c", a=8, b=8, s=5)
+                    col = 16 * e + j
+                    for s in range(5):
+                        src = W[:, 8 * e + ROW0[s] : 8 * e + ROW0[s] + 8, 8 * j + COL0[s] : 8 * j + COL0[s] + 8, :]
+                        if s in V_SHIFTS[e]:
+                            nc.vector.tensor_scalar(
+                                out=nbv[:, :, :, s, :], in0=src,
+                                scalar1=rstd[:, col : col + 1], scalar2=nbias[:, col : col + 1],
+                                op0=ALU.mult, op1=ALU.add,
+                            )
+                        else:
+                            nc.scalar.activation(
+                                out=nbv[:, :, :, s, :], in_=src, func=ACT.Identity,
+                                scale=rstd[:, col : col + 1], bias=nbias[:, col : col + 1],
+                            )
+                    nbs.append(nb)
+                zc = cpool.tile([P, 5, 256], U32, name="zc", align_bytes=64)
+                zs = cpool.tile([P, 5, 256], U8, name="zs", align_bytes=64)
+                for g5 in range(5):
+                    zp = zpool.tile([P, 4, 256], BF16, name="zp")
+                    for half in range(2):
+                        pt = pst.tile([P, 2, 2, P], F32, name="pt")
+                        for a in range(2):
+                            sl = 4 * g5 + 2 * half + a
+                            for u in range(2):
+                                nc.tensor.transpose(pt[:, a, u, :], nbs[u][:, P * sl : P * sl + P], ident[:])
+                        for a in range(2):
+                            sl = 4 * g5 + 2 * half + a
+                            nc.scalar.activation(
+                                out=zp[:, 2 * half + a, :], in_=pt[:, a, :, :].rearrange("p u r -> p (u r)"),
+                                func=ACT.Identity, scale=gb[:, sl : sl + 1], bias=gb[:, 32 + sl : 33 + sl],
+                            )
+                    zi = zpool.tile([P, 256, 4], BF16, name="zi", align_bytes=64)
+                    nc.vector.tensor_copy(
+                        out=zi[:].rearrange("p (c i) t -> p c t i", i=4),
+                        in_=zp[:].rearrange("p t (c i) -> p c t i", i=4),
+                    )
+                    nc.vector.quantize_mx(
+                        out=zc[:, g5, :].bitcast(FP8X4), scales=zs[:, g5, :], in_=zi[:].rearrange("p c t -> p (c t)")
+                    )
+                ot = iopool.tile([P, 2, DIM], F32, name="ot")
+                for u in range(2):
+                    acc = psm.tile([P, DIM], F32, name="acc")
+                    for g5 in range(5):
+                        nc.tensor.matmul_mx(
+                            out=acc[:],
+                            lhsT=zc[:, g5, P * u : P * u + P].bitcast(FP8X4),
+                            lhsT_scale=zs[:, g5, P * u : P * u + P],
+                            rhs=wc[:, g5, :].bitcast(FP8X4),
+                            rhs_scale=ws[:, g5, :],
+                            start=(g5 == 0),
+                            stop=(g5 == 4),
+                        )
+                    nc.vector.tensor_tensor(out=ot[:, u, :], in0=acc[:], in1=tb[:, u, :], op=ALU.add)
+                nc.sync.dma_start(out=out_v[:, :, j, :], in_=ot[:])

@@ -1,8 +1,6 @@
 from contextlib import ExitStack
 
-import concourse.bass as bass
 import concourse.mybir as mybir
-import concourse.tile as tile
 from concourse.masks import make_identity
 
 F32 = mybir.dt.float32
@@ -12,6 +10,7 @@ U8 = mybir.dt.uint8
 FP8X4 = mybir.dt.float8_e4m3fn_x4
 ALU = mybir.AluOpType
 ACT = mybir.ActivationFunctionType
+AX = mybir.AxisListType
 
 P = 128
 KDIM = 2560
@@ -20,12 +19,12 @@ FLOPS = 2 * 4096 * KDIM * DIM
 
 ROW0 = (4, 0, 0, 8, 8)
 COL0 = (4, 0, 8, 0, 8)
-V_SHIFTS = ((0, 1, 2, 3), (0, 1, 2))
+S_SLOTS = (1, 5, 9)
 
 
 def tile_shiftedpatchtokenization_pb_t_kernel(tc, x, ln2_g, ln2_b, w2, b2, tok, out):
     nc = tc.nc
-    xv = x.rearrange("b c (g q r) w -> g q b c (r w)", g=8, q=4)
+    xv = x.rearrange("b c (g u r) w -> (b c) g u (r w)", g=8, u=8)
     wv = w2.rearrange("(g t p) n -> g p t n", t=4, p=P)
     tok_v = tok.rearrange("b (g e j) d -> (b g) e j d", g=8, e=2)
     out_v = out.rearrange("b (g e j) d -> (b g) e j d", g=8, e=2)
@@ -53,36 +52,48 @@ def tile_shiftedpatchtokenization_pb_t_kernel(tc, x, ln2_g, ln2_b, w2, b2, tok, 
         rstd = keep.tile([P, 32], F32)
         nbias = keep.tile([P, 32], F32)
         one = keep.tile([P, 1], F32)
+        mask_top = keep.tile([P, 1], F32)
+        mask_bot = keep.tile([P, 1], F32)
 
         nc.vector.memset(one[:], 1.0)
         nc.scalar.sqrt(one[:], one[:])
 
         make_identity(nc, ident[:])
+        id8 = ident[:].rearrange("p (a b) -> p a b", b=8)
         nc.vector.memset(sh_dn[:], 0.0)
         nc.vector.memset(sh_up[:], 0.0)
         nc.vector.tensor_copy(out=sh_dn[:, 1:P], in_=ident[:, 0 : P - 1])
         nc.vector.tensor_copy(out=sh_up[:, 0 : P - 1], in_=ident[:, 1:P])
         nc.vector.memset(sh_dn[:].rearrange("p (a b) -> p a b", b=8)[:, :, 0:1], 0.0)
         nc.vector.memset(sh_up[:].rearrange("p (a b) -> p a b", b=8)[:, :, 7:8], 0.0)
+        nc.vector.tensor_reduce(out=mask_top[:], in_=id8[:, :, 0], axis=AX.X, op=ALU.add)
+        nc.vector.tensor_reduce(out=mask_bot[:], in_=id8[:, :, 7], axis=AX.X, op=ALU.add)
+        nc.vector.tensor_scalar(out=mask_top[:], in0=mask_top[:], scalar1=-1.0, scalar2=1.0, op0=ALU.mult, op1=ALU.add)
+        nc.vector.tensor_scalar(out=mask_bot[:], in0=mask_bot[:], scalar1=-1.0, scalar2=1.0, op0=ALU.mult, op1=ALU.add)
         nc.vector.memset(W[:, :, 0:4, :], 0.0)
         nc.vector.memset(W[:, :, 132:136, :], 0.0)
         nc.vector.memset(CR[:], 0.0)
 
         with ExitStack() as pa:
-            xpool = pa.enter_context(tc.tile_pool(name="xpool", bufs=2))
+            xpool = pa.enter_context(tc.tile_pool(name="xpool", bufs=3))
+            hpool = pa.enter_context(tc.tile_pool(name="hpool", bufs=2))
             tpool = pa.enter_context(tc.tile_pool(name="tpool", bufs=1))
-            wpool = pa.enter_context(tc.tile_pool(name="wpool", bufs=2))
-            psa = pa.enter_context(tc.psum_pool(name="psa", bufs=2))
+            psa = pa.enter_context(tc.psum_pool(name="psa", bufs=3))
+            psx = pa.enter_context(tc.psum_pool(name="psx", bufs=2))
 
             junk = tpool.tile([P, 4, 4, 8], F32)
+            m_a = tpool.tile([P, 2056], F32)
+            m_b = tpool.tile([P, 2056], F32)
+            for m_t in (m_a, m_b):
+                nc.vector.memset(m_t[:, 0:4], 0.0)
+                nc.vector.memset(m_t[:, 2052:2056], 0.0)
 
-            def load_chunk(q):
-                xs = xpool.tile([P, 8, 2048], BF16, name="xs")
-                for g in (0, 4, 1, 5, 2, 6, 3, 7):
-                    nc.sync.dma_start(out=xs[g:P:8, :, :], in_=xv[g, q])
+            def load_chunk(u):
+                xs = xpool.tile([P, 8, 1024], BF16, name="xs")
+                nc.sync.dma_start(out=xs[:], in_=xv[:, :, u, :])
                 return xs
 
-            xs_next = load_chunk(0)
+            xs_q = [load_chunk(0), load_chunk(1)]
 
             g0b = tpool.tile([P, P], BF16)
             g0f = tpool.tile([P, P], F32)
@@ -91,59 +102,76 @@ def tile_shiftedpatchtokenization_pb_t_kernel(tc, x, ln2_g, ln2_b, w2, b2, tok, 
             nc.sync.dma_start(out=g0b[32:52, :], in_=ln2_b.rearrange("(s p) -> s p", p=P))
             nc.sync.dma_start(out=b2bc[:], in_=b2.partition_broadcast(P))
             nc.vector.tensor_copy(out=g0f[:], in_=g0b[:])
-            gps = psa.tile([P, P], F32, name="gps")
+            gps = psx.tile([P, P], F32, name="gps", tag="misc")
             nc.tensor.transpose(gps[:], g0f[:], ident[:])
             nc.vector.tensor_copy(out=gb[:], in_=gps[:])
 
-            for q in range(4):
-                xs = xs_next
-                if q < 3:
-                    xs_next = load_chunk(q + 1)
-                if q == 0:
+            for u in range(8):
+                xs = xs_q[u]
+                if u + 2 < 8:
+                    xs_q.append(load_chunk(u + 2))
+                xq = xs[:].rearrange("p g (o e x f) -> p g o e x f", o=2, e=2, x=128, f=2)
+                h = hpool.tile([P, 8, 2, 128], F32, name="h")
+                nc.vector.scalar_tensor_tensor(
+                    out=h[:], in0=xq[:, :, :, 0, :, 0], scalar=3.0, in1=xq[:, :, :, 0, :, 1],
+                    op0=ALU.mult, op1=ALU.subtract,
+                )
+                nc.vector.tensor_tensor(out=h[:], in0=h[:], in1=xq[:, :, :, 1, :, 0], op=ALU.subtract)
+                nc.vector.tensor_tensor(out=h[:], in0=h[:], in1=xq[:, :, :, 1, :, 1], op=ALU.subtract)
+                m_t = m_a if u % 2 == 0 else m_b
+                m_v = m_t[:, 4:2052].rearrange("p (c o b g) -> p c o b g", c=8, o=2, b=16)
+                for o in range(2):
+                    for hq in range(2):
+                        p1 = psa.tile([P, 4, P], F32, name="p1")
+                        for gq in range(4):
+                            nc.tensor.transpose(p1[:, gq, :], h[:, 4 * hq + gq, o, :], ident[:])
+                        nc.scalar.copy(
+                            out=m_v[:, :, o, :, 4 * hq : 4 * hq + 4],
+                            in_=p1[:].rearrange("p q (b c) -> p c b q", c=8),
+                        )
+                for o in range(2):
+                    ro = 2 * u + o
+                    jobs = [(4 + ro, 0, None)]
+                    if ro < 4:
+                        jobs.append((20 + ro, 1, mask_bot))
+                    if ro >= 12:
+                        jobs.append((ro - 12, -1, mask_top))
+                    for r, shift, mask in jobs:
+                        for ch in range(2):
+                            p2 = psa.tile([P, 4, P], F32, name="p2")
+                            for c4 in range(4):
+                                base = 4 + ((4 * ch + c4) * 2 + o) * P + shift
+                                nc.tensor.transpose(p2[:, c4, :], m_t[:, base : base + P], ident[:])
+                            dst = W[:, r, 4:132, 4 * ch : 4 * ch + 4]
+                            srcv = p2[:].rearrange("p c x -> p x c")
+                            if mask is None:
+                                nc.vector.tensor_copy(out=dst, in_=srcv)
+                            else:
+                                nc.vector.tensor_scalar(
+                                    out=dst, in0=srcv, scalar1=mask[:, 0:1], scalar2=None, op0=ALU.mult
+                                )
+                if u == 1:
                     for g5 in range(5):
-                        wraw = wpool.tile([P, 4, DIM], BF16, name="wraw")
+                        wraw = tpool.tile([P, 4, DIM], BF16, name="wraw")
                         nc.sync.dma_start(out=wraw[:], in_=wv[g5])
-                        wgrp = wpool.tile([P, DIM, 4], BF16, name="wgrp", align_bytes=64)
+                        wgrp = tpool.tile([P, DIM, 4], BF16, name="wgrp", align_bytes=64)
                         nc.scalar.copy(out=wgrp[:], in_=wraw[:].rearrange("p t n -> p n t"))
                         nc.vector.quantize_mx(
                             out=wc[:, g5, :].bitcast(FP8X4),
                             scales=ws[:, g5, :],
                             in_=wgrp[:].rearrange("p n t -> p (n t)"),
                         )
-                xq = xs[:].rearrange("p c (y e x f) -> p c y e x f", y=4, e=2, x=128, f=2)
-                t = tpool.tile([P, 8, 4, 128], F32, name="t")
-                nc.vector.scalar_tensor_tensor(
-                    out=t[:], in0=xq[:, :, :, 0, :, 0], scalar=3.0, in1=xq[:, :, :, 0, :, 1],
-                    op0=ALU.mult, op1=ALU.subtract,
-                )
-                nc.vector.tensor_tensor(out=t[:], in0=t[:], in1=xq[:, :, :, 1, :, 0], op=ALU.subtract)
-                r0 = 4 + 4 * q
-                nc.vector.tensor_tensor(
-                    out=W[:, r0 : r0 + 4, 4:132, :],
-                    in0=t[:].rearrange("p c y x -> p y x c"),
-                    in1=xq[:, :, :, 1, :, 1].rearrange("p c y x -> p y x c"),
-                    op=ALU.subtract,
-                )
-                for cx in range(32):
-                    cell = W[:, r0 : r0 + 4, 4 + 4 * cx : 8 + 4 * cx, :]
-                    nc.scalar.activation(out=junk[:], in_=cell, func=ACT.Identity, accum_out=CS[:, 0, q, cx : cx + 1])
-                    nc.scalar.activation(out=junk[:], in_=cell, func=ACT.Square, accum_out=CS[:, 1, q, cx : cx + 1])
-                if q == 0 or q == 3:
-                    sh = sh_up if q == 0 else sh_dn
-                    dst0 = 20 if q == 0 else 0
-                    for y in range(4):
-                        for h in range(2):
-                            hp = psa.tile([P, 512], F32, name="hp")
-                            cols = slice(4 + 64 * h, 68 + 64 * h)
-                            nc.tensor.matmul(
-                                out=hp[:], lhsT=sh[:], rhs=W[:, r0 + y, cols, :].rearrange("p x c -> p (x c)"),
-                                start=True, stop=True,
-                            )
-                            nc.vector.tensor_copy(out=W[:, dst0 + y, cols, :].rearrange("p x c -> p (x c)"), in_=hp[:])
+                if u % 2 == 1:
+                    q = u // 2
+                    r0 = 4 + 4 * q
+                    for cx in range(32):
+                        cell = W[:, r0 : r0 + 4, 4 + 4 * cx : 8 + 4 * cx, :]
+                        nc.scalar.activation(out=junk[:], in_=cell, func=ACT.Identity, accum_out=CS[:, 0, q, cx : cx + 1])
+                        nc.scalar.activation(out=junk[:], in_=cell, func=ACT.Square, accum_out=CS[:, 1, q, cx : cx + 1])
 
             cs_flat = CS[:].rearrange("p k q x -> p (k q x)")
-            pdn = psa.tile([P, 2, 4, 32], F32, name="pdn")
-            pup = psa.tile([P, 2, 4, 32], F32, name="pup")
+            pdn = psx.tile([P, 2, 4, 32], F32, name="pdn", tag="misc")
+            pup = psx.tile([P, 2, 4, 32], F32, name="pup", tag="misc")
             nc.tensor.matmul(out=pdn[:].rearrange("p k q x -> p (k q x)"), lhsT=sh_dn[:], rhs=cs_flat, start=True, stop=True)
             nc.tensor.matmul(out=pup[:].rearrange("p k q x -> p (k q x)"), lhsT=sh_up[:], rhs=cs_flat, start=True, stop=True)
             nc.vector.tensor_copy(out=CR[:, :, 1:5, 1:33], in_=CS[:])
@@ -172,63 +200,57 @@ def tile_shiftedpatchtokenization_pb_t_kernel(tc, x, ln2_g, ln2_b, w2, b2, tok, 
             )
 
         with ExitStack() as pb:
-            npool = pb.enter_context(tc.tile_pool(name="npool", bufs=5))
+            npool = pb.enter_context(tc.tile_pool(name="npool", bufs=4))
             zpool = pb.enter_context(tc.tile_pool(name="zpool", bufs=3))
             cpool = pb.enter_context(tc.tile_pool(name="cpool", bufs=2))
             iopool = pb.enter_context(tc.tile_pool(name="iopool", bufs=3))
-            pst = pb.enter_context(tc.psum_pool(name="pst", bufs=5))
+            pst = pb.enter_context(tc.psum_pool(name="pst", bufs=6))
             psm = pb.enter_context(tc.psum_pool(name="psm", bufs=2))
+            pb.enter_context(tc.manual_schedule())
 
-            for j in range(16):
+            nbs = {}
+            tbs = {}
+            codes = {}
+            zis = {}
+
+            def load(r):
                 tk = iopool.tile([P, 2, DIM], BF16, name="tk")
-                nc.sync.dma_start(out=tk[:], in_=tok_v[:, :, j, :])
+                nc.sync.dma_start(out=tk[:], in_=tok_v[:, :, r, :])
                 tb = iopool.tile([P, 2, DIM], F32, name="tb")
                 for e in range(2):
                     nc.gpsimd.tensor_tensor(out=tb[:, e, :], in0=tk[:, e, :], in1=b2bc[:], op=ALU.add)
-                nbs = []
-                for e in range(2):
-                    nb = npool.tile([P, KDIM], F32, name="nb")
-                    nbv = nb[:].rearrange("p (a b s c) -> p a b s c", a=8, b=8, s=5)
-                    col = 16 * e + j
-                    for s in range(5):
-                        src = W[:, 8 * e + ROW0[s] : 8 * e + ROW0[s] + 8, 8 * j + COL0[s] : 8 * j + COL0[s] + 8, :]
-                        if s in V_SHIFTS[e]:
-                            nc.vector.tensor_scalar(
-                                out=nbv[:, :, :, s, :], in0=src,
-                                scalar1=rstd[:, col : col + 1], scalar2=nbias[:, col : col + 1],
-                                op0=ALU.mult, op1=ALU.add,
-                            )
-                        else:
-                            nc.scalar.activation(
-                                out=nbv[:, :, :, s, :], in_=src, func=ACT.Identity,
-                                scale=rstd[:, col : col + 1], bias=nbias[:, col : col + 1],
-                            )
-                    nbs.append(nb)
-                zc = cpool.tile([P, 5, 256], U32, name="zc", align_bytes=64)
-                zs = cpool.tile([P, 5, 256], U8, name="zs", align_bytes=64)
-                for g5 in range(5):
-                    zp = zpool.tile([P, 4, 256], BF16, name="zp")
-                    for half in range(2):
-                        pt = pst.tile([P, 2, 2, P], F32, name="pt")
-                        for a in range(2):
-                            sl = 4 * g5 + 2 * half + a
-                            for u in range(2):
-                                nc.tensor.transpose(pt[:, a, u, :], nbs[u][:, P * sl : P * sl + P], ident[:])
-                        for a in range(2):
-                            sl = 4 * g5 + 2 * half + a
-                            nc.scalar.activation(
-                                out=zp[:, 2 * half + a, :], in_=pt[:, a, :, :].rearrange("p u r -> p (u r)"),
-                                func=ACT.Identity, scale=gb[:, sl : sl + 1], bias=gb[:, 32 + sl : 33 + sl],
-                            )
-                    zi = zpool.tile([P, 256, 4], BF16, name="zi", align_bytes=64)
-                    nc.vector.tensor_copy(
-                        out=zi[:].rearrange("p (c i) t -> p c t i", i=4),
-                        in_=zp[:].rearrange("p t (c i) -> p c t i", i=4),
+                tbs[r] = tb
+
+            def norm(r, slot):
+                e, s = divmod(slot, 5)
+                if s == 0:
+                    nbs[(r, e)] = npool.tile([P, KDIM], F32, name="nb")
+                nbv = nbs[(r, e)][:].rearrange("p (a b s c) -> p a b s c", a=8, b=8, s=5)
+                col = 16 * e + r
+                srcw = W[:, 8 * e + ROW0[s] : 8 * e + ROW0[s] + 8, 8 * r + COL0[s] : 8 * r + COL0[s] + 8, :]
+                if slot in S_SLOTS:
+                    nc.scalar.activation(
+                        out=nbv[:, :, :, s, :], in_=srcw, func=ACT.Identity,
+                        scale=rstd[:, col : col + 1], bias=nbias[:, col : col + 1],
                     )
-                    nc.vector.quantize_mx(
-                        out=zc[:, g5, :].bitcast(FP8X4), scales=zs[:, g5, :], in_=zi[:].rearrange("p c t -> p (c t)")
+                else:
+                    nc.vector.tensor_scalar(
+                        out=nbv[:, :, :, s, :], in0=srcw,
+                        scalar1=rstd[:, col : col + 1], scalar2=nbias[:, col : col + 1],
+                        op0=ALU.mult, op1=ALU.add,
                     )
+
+            def quantise(r, g5):
+                zc, zs = codes[r]
+                nc.vector.quantize_mx(
+                    out=zc[:, g5, :].bitcast(FP8X4), scales=zs[:, g5, :],
+                    in_=zis[(r, g5)][:].rearrange("p c t -> p (c t)"),
+                )
+
+            def project(r):
+                zc, zs = codes[r]
                 ot = iopool.tile([P, 2, DIM], F32, name="ot")
+                accs = []
                 for u in range(2):
                     acc = psm.tile([P, DIM], F32, name="acc")
                     for g5 in range(5):
@@ -241,5 +263,46 @@ def tile_shiftedpatchtokenization_pb_t_kernel(tc, x, ln2_g, ln2_b, w2, b2, tok, 
                             start=(g5 == 0),
                             stop=(g5 == 4),
                         )
-                    nc.vector.tensor_tensor(out=ot[:, u, :], in0=acc[:], in1=tb[:, u, :], op=ALU.add)
-                nc.sync.dma_start(out=out_v[:, :, j, :], in_=ot[:])
+                    accs.append(acc)
+                for u in range(2):
+                    nc.vector.tensor_tensor(out=ot[:, u, :], in0=accs[u][:], in1=tbs[r][:, u, :], op=ALU.add)
+                nc.sync.dma_start(out=out_v[:, :, r, :], in_=ot[:])
+
+            load(0)
+            for slot in range(10):
+                norm(0, slot)
+            for r in range(16):
+                if r + 1 < 16:
+                    load(r + 1)
+                zc_t = cpool.tile([P, 5, 256], U32, name="zc", align_bytes=64)
+                zs_t = cpool.tile([P, 5, 256], U8, name="zs", align_bytes=64)
+                codes[r] = (zc_t, zs_t)
+                for g5 in range(5):
+                    zp = zpool.tile([P, 4, 256], BF16, name="zp")
+                    for half in range(2):
+                        pt = pst.tile([P, 2, 2, P], F32, name="pt")
+                        for a in range(2):
+                            sl = 4 * g5 + 2 * half + a
+                            for u in range(2):
+                                nc.tensor.transpose(pt[:, a, u, :], nbs[(r, u)][:, P * sl : P * sl + P], ident[:])
+                        for a in range(2):
+                            sl = 4 * g5 + 2 * half + a
+                            nc.scalar.activation(
+                                out=zp[:, 2 * half + a, :], in_=pt[:, a, :, :].rearrange("p u r -> p (u r)"),
+                                func=ACT.Identity, scale=gb[:, sl : sl + 1], bias=gb[:, 32 + sl : 33 + sl],
+                            )
+                    if r + 1 < 16:
+                        norm(r + 1, 2 * g5)
+                        norm(r + 1, 2 * g5 + 1)
+                    zi = zpool.tile([P, 256, 4], BF16, name="zi", align_bytes=64)
+                    zis[(r, g5)] = zi
+                    nc.vector.tensor_copy(
+                        out=zi[:].rearrange("p (c i) t -> p c t i", i=4),
+                        in_=zp[:].rearrange("p t (c i) -> p c t i", i=4),
+                    )
+                    if g5 >= 1:
+                        quantise(r, g5 - 1)
+                quantise(r, 4)
+                if r >= 1:
+                    project(r - 1)
+            project(15)

@@ -20,6 +20,7 @@ FLOPS = 2 * 4096 * KDIM * DIM
 ROW0 = (4, 0, 0, 8, 8)
 COL0 = (4, 0, 8, 0, 8)
 S_SLOTS = (1, 5, 9)
+ORDER = (6, 7, 0, 1, 2, 3, 4, 5)
 
 
 def tile_shiftedpatchtokenization_pb_t_kernel(tc, x, ln2_g, ln2_b, w2, b2, tok, out):
@@ -73,6 +74,7 @@ def tile_shiftedpatchtokenization_pb_t_kernel(tc, x, ln2_g, ln2_b, w2, b2, tok, 
         nc.vector.memset(W[:, :, 0:4, :], 0.0)
         nc.vector.memset(W[:, :, 132:136, :], 0.0)
         nc.vector.memset(CR[:], 0.0)
+        nc.vector.memset(CS[:], 0.0)
 
         with ExitStack() as pa:
             xpool = pa.enter_context(tc.tile_pool(name="xpool", bufs=3))
@@ -81,36 +83,32 @@ def tile_shiftedpatchtokenization_pb_t_kernel(tc, x, ln2_g, ln2_b, w2, b2, tok, 
             psa = pa.enter_context(tc.psum_pool(name="psa", bufs=3))
             psx = pa.enter_context(tc.psum_pool(name="psx", bufs=2))
 
-            junk = tpool.tile([P, 4, 4, 8], F32)
             m_a = tpool.tile([P, 2056], F32)
             m_b = tpool.tile([P, 2056], F32)
             for m_t in (m_a, m_b):
                 nc.vector.memset(m_t[:, 0:4], 0.0)
                 nc.vector.memset(m_t[:, 2052:2056], 0.0)
-
-            def load_chunk(u):
-                xs = xpool.tile([P, 8, 1024], BF16, name="xs")
-                nc.sync.dma_start(out=xs[:], in_=xv[:, :, u, :])
-                return xs
-
-            xs_q = [load_chunk(0), load_chunk(1)]
-
             g0b = tpool.tile([P, P], BF16)
             g0f = tpool.tile([P, P], F32)
             nc.vector.memset(g0b[:], 0.0)
-            nc.sync.dma_start(out=g0b[0:20, :], in_=ln2_g.rearrange("(s p) -> s p", p=P))
-            nc.sync.dma_start(out=g0b[32:52, :], in_=ln2_b.rearrange("(s p) -> s p", p=P))
-            nc.sync.dma_start(out=b2bc[:], in_=b2.partition_broadcast(P))
-            nc.vector.tensor_copy(out=g0f[:], in_=g0b[:])
-            gps = psx.tile([P, P], F32, name="gps", tag="misc")
-            nc.tensor.transpose(gps[:], g0f[:], ident[:])
-            nc.vector.tensor_copy(out=gb[:], in_=gps[:])
+            bns = tpool.tile([P, 4, 32, 6], F32)
+            sq_a = tpool.tile([P, 32], F32)
+            sq_b = tpool.tile([P, 32], F32)
+            wpool = pa.enter_context(tc.tile_pool(name="wpool", bufs=2))
+            wraws = {}
+            wgrps = {}
 
-            for u in range(8):
-                xs = xs_q[u]
-                if u + 2 < 8:
-                    xs_q.append(load_chunk(u + 2))
-                xq = xs[:].rearrange("p g (o e x f) -> p g o e x f", o=2, e=2, x=128, f=2)
+            pa.enter_context(tc.manual_schedule())
+            xss = {}
+            hs = {}
+
+            def load_chunk(i):
+                xs = xpool.tile([P, 8, 1024], BF16, name="xs")
+                nc.sync.dma_start(out=xs[:], in_=xv[:, :, ORDER[i], :])
+                xss[i] = xs
+
+            def haar(i):
+                xq = xss[i][:].rearrange("p g (o e x f) -> p g o e x f", o=2, e=2, x=128, f=2)
                 h = hpool.tile([P, 8, 2, 128], F32, name="h")
                 nc.vector.scalar_tensor_tensor(
                     out=h[:], in0=xq[:, :, :, 0, :, 0], scalar=3.0, in1=xq[:, :, :, 0, :, 1],
@@ -118,7 +116,12 @@ def tile_shiftedpatchtokenization_pb_t_kernel(tc, x, ln2_g, ln2_b, w2, b2, tok, 
                 )
                 nc.vector.tensor_tensor(out=h[:], in0=h[:], in1=xq[:, :, :, 1, :, 0], op=ALU.subtract)
                 nc.vector.tensor_tensor(out=h[:], in0=h[:], in1=xq[:, :, :, 1, :, 1], op=ALU.subtract)
-                m_t = m_a if u % 2 == 0 else m_b
+                hs[i] = h
+
+            def relayout(i):
+                u = ORDER[i]
+                h = hs[i]
+                m_t = m_a if i % 2 == 0 else m_b
                 m_v = m_t[:, 4:2052].rearrange("p (c o b g) -> p c o b g", c=8, o=2, b=16)
                 for o in range(2):
                     for hq in range(2):
@@ -145,38 +148,71 @@ def tile_shiftedpatchtokenization_pb_t_kernel(tc, x, ln2_g, ln2_b, w2, b2, tok, 
                             dst = W[:, r, 4:132, 4 * ch : 4 * ch + 4]
                             srcv = p2[:].rearrange("p c x -> p x c")
                             if mask is None:
-                                nc.vector.tensor_copy(out=dst, in_=srcv)
+                                nc.scalar.copy(out=dst, in_=srcv)
                             else:
-                                nc.vector.tensor_scalar(
-                                    out=dst, in0=srcv, scalar1=mask[:, 0:1], scalar2=None, op0=ALU.mult
-                                )
-                if u == 1:
-                    for g5 in range(5):
-                        wraw = tpool.tile([P, 4, DIM], BF16, name="wraw")
-                        nc.sync.dma_start(out=wraw[:], in_=wv[g5])
-                        wgrp = tpool.tile([P, DIM, 4], BF16, name="wgrp", align_bytes=64)
-                        nc.scalar.copy(out=wgrp[:], in_=wraw[:].rearrange("p t n -> p n t"))
-                        nc.vector.quantize_mx(
-                            out=wc[:, g5, :].bitcast(FP8X4),
-                            scales=ws[:, g5, :],
-                            in_=wgrp[:].rearrange("p n t -> p (n t)"),
-                        )
-                if u % 2 == 1:
-                    q = u // 2
-                    r0 = 4 + 4 * q
-                    for cx in range(32):
-                        cell = W[:, r0 : r0 + 4, 4 + 4 * cx : 8 + 4 * cx, :]
-                        nc.scalar.activation(out=junk[:], in_=cell, func=ACT.Identity, accum_out=CS[:, 0, q, cx : cx + 1])
-                        nc.scalar.activation(out=junk[:], in_=cell, func=ACT.Square, accum_out=CS[:, 1, q, cx : cx + 1])
+                                nc.scalar.activation(out=dst, in_=srcv, func=ACT.Copy, scale=mask[:, 0:1])
 
-            cs_flat = CS[:].rearrange("p k q x -> p (k q x)")
-            pdn = psx.tile([P, 2, 4, 32], F32, name="pdn", tag="misc")
-            pup = psx.tile([P, 2, 4, 32], F32, name="pup", tag="misc")
-            nc.tensor.matmul(out=pdn[:].rearrange("p k q x -> p (k q x)"), lhsT=sh_dn[:], rhs=cs_flat, start=True, stop=True)
-            nc.tensor.matmul(out=pup[:].rearrange("p k q x -> p (k q x)"), lhsT=sh_up[:], rhs=cs_flat, start=True, stop=True)
-            nc.vector.tensor_copy(out=CR[:, :, 1:5, 1:33], in_=CS[:])
-            nc.vector.tensor_copy(out=CR[:, :, 0, 1:33], in_=pdn[:, :, 3, :])
-            nc.vector.tensor_copy(out=CR[:, :, 5, 1:33], in_=pup[:, :, 0, :])
+            def cell_sums(q):
+                r0 = 4 + 4 * q
+                for cx in range(32):
+                    nc.vector.bn_stats(out=bns[:, q, cx, :], in_=W[:, r0 : r0 + 4, 4 + 4 * cx : 8 + 4 * cx, :])
+                nc.vector.tensor_tensor(out=CS[:, 0, q, :], in0=bns[:, q, :, 1], in1=bns[:, q, :, 4], op=ALU.add)
+                nc.vector.tensor_tensor(out=sq_a[:], in0=bns[:, q, :, 1], in1=bns[:, q, :, 1], op=ALU.mult)
+                nc.vector.tensor_tensor(out=sq_b[:], in0=bns[:, q, :, 4], in1=bns[:, q, :, 4], op=ALU.mult)
+                nc.vector.tensor_tensor(out=sq_a[:], in0=sq_a[:], in1=sq_b[:], op=ALU.add)
+                nc.vector.tensor_tensor(out=sq_b[:], in0=bns[:, q, :, 2], in1=bns[:, q, :, 5], op=ALU.add)
+                nc.vector.scalar_tensor_tensor(
+                    out=CS[:, 1, q, :], in0=sq_a[:], scalar=64.0, in1=sq_b[:], op0=ALU.mult, op1=ALU.add
+                )
+                nc.vector.tensor_copy(out=CR[:, :, 1 + q, 1:33], in_=CS[:, :, q, :])
+
+            for i in range(3):
+                load_chunk(i)
+            nc.sync.dma_start(out=g0b[0:20, :], in_=ln2_g.rearrange("(s p) -> s p", p=P))
+            nc.sync.dma_start(out=g0b[32:52, :], in_=ln2_b.rearrange("(s p) -> s p", p=P))
+            nc.sync.dma_start(out=b2bc[:], in_=b2.partition_broadcast(P))
+
+            def load_w(g5):
+                wraws[g5] = wpool.tile([P, 4, DIM], BF16, name="wraw")
+                nc.sync.dma_start(out=wraws[g5][:], in_=wv[g5])
+
+            load_w(0)
+            load_w(1)
+
+            for i in range(10):
+                if i < 8:
+                    haar(i)
+                    if i + 3 < 8:
+                        load_chunk(i + 3)
+                if i == 0:
+                    nc.vector.tensor_copy(out=g0f[:], in_=g0b[:])
+                    gps = psx.tile([P, P], F32, name="gps", tag="misc")
+                    nc.tensor.transpose(gps[:], g0f[:], ident[:])
+                    nc.vector.tensor_copy(out=gb[:], in_=gps[:])
+                if i == 6:
+                    cs_flat = CS[:].rearrange("p k q x -> p (k q x)")
+                    pdn = psx.tile([P, 2, 4, 32], F32, name="pdn", tag="misc")
+                    pup = psx.tile([P, 2, 4, 32], F32, name="pup", tag="misc")
+                    nc.tensor.matmul(out=pdn[:].rearrange("p k q x -> p (k q x)"), lhsT=sh_dn[:], rhs=cs_flat, start=True, stop=True)
+                    nc.tensor.matmul(out=pup[:].rearrange("p k q x -> p (k q x)"), lhsT=sh_up[:], rhs=cs_flat, start=True, stop=True)
+                    nc.vector.tensor_copy(out=CR[:, :, 0, 1:33], in_=pdn[:, :, 3, :])
+                    nc.vector.tensor_copy(out=CR[:, :, 5, 1:33], in_=pup[:, :, 0, :])
+                if 1 <= i <= 8:
+                    relayout(i - 1)
+                if 1 <= i <= 5:
+                    wgrps[i - 1] = wpool.tile([P, DIM, 4], BF16, name="wgrp", align_bytes=64)
+                    nc.scalar.copy(out=wgrps[i - 1][:], in_=wraws[i - 1][:].rearrange("p t n -> p n t"))
+                    if i + 1 < 5:
+                        load_w(i + 1)
+                if 2 <= i <= 6:
+                    nc.vector.quantize_mx(
+                        out=wc[:, i - 2, :].bitcast(FP8X4),
+                        scales=ws[:, i - 2, :],
+                        in_=wgrps[i - 2][:].rearrange("p n t -> p (n t)"),
+                    )
+                if i >= 3 and i % 2 == 1:
+                    cell_sums(ORDER[i - 3] // 2)
+
             nc.vector.tensor_tensor(out=A1[:], in0=CR[:, :, 0:5, :], in1=CR[:, :, 1:6, :], op=ALU.add)
             nc.vector.tensor_tensor(out=Rw[:], in0=A1[:, :, 0:3:2, :], in1=A1[:, :, 2:5:2, :], op=ALU.add)
             nc.vector.tensor_tensor(out=Bw[:], in0=Rw[:, :, :, 0:33], in1=Rw[:, :, :, 1:34], op=ALU.add)
@@ -185,7 +221,7 @@ def tile_shiftedpatchtokenization_pb_t_kernel(tc, x, ln2_g, ln2_b, w2, b2, tok, 
             nc.vector.tensor_tensor(out=ST[:], in0=ST[:], in1=Bc[:, :, :, 1:32:2], op=ALU.add)
             s1 = ST[:, 0, :, :].rearrange("p e j -> p (e j)")
             s2 = ST[:, 1, :, :].rearrange("p e j -> p (e j)")
-            nc.vector.tensor_scalar(out=mean[:], in0=s1, scalar1=1.0 / KDIM, scalar2=None, op0=ALU.mult)
+            nc.vector.tensor_scalar(out=mean[:], in0=s1, scalar1=64.0 / KDIM, scalar2=None, op0=ALU.mult)
             nc.vector.tensor_tensor(out=tmp[:], in0=mean[:], in1=mean[:], op=ALU.mult)
             nc.vector.tensor_scalar(out=va[:], in0=s2, scalar1=1.0 / KDIM, scalar2=36.0e-5, op0=ALU.mult, op1=ALU.add)
             nc.vector.tensor_tensor(out=va[:], in0=va[:], in1=tmp[:], op=ALU.subtract)
@@ -210,15 +246,19 @@ def tile_shiftedpatchtokenization_pb_t_kernel(tc, x, ln2_g, ln2_b, w2, b2, tok, 
 
             nbs = {}
             tbs = {}
+            tks = {}
             codes = {}
             zis = {}
 
             def load(r):
-                tk = iopool.tile([P, 2, DIM], BF16, name="tk")
-                nc.sync.dma_start(out=tk[:], in_=tok_v[:, :, r, :])
+                tks[r] = iopool.tile([P, 2, DIM], BF16, name="tk")
+                nc.sync.dma_start(out=tks[r][:], in_=tok_v[:, :, r, :])
+
+            def add_bias(r):
                 tb = iopool.tile([P, 2, DIM], F32, name="tb")
-                for e in range(2):
-                    nc.gpsimd.tensor_tensor(out=tb[:, e, :], in0=tk[:, e, :], in1=b2bc[:], op=ALU.add)
+                nc.vector.tensor_tensor(
+                    out=tb[:], in0=tks[r][:], in1=b2bc[:].unsqueeze(1).to_broadcast([P, 2, DIM]), op=ALU.add
+                )
                 tbs[r] = tb
 
             def norm(r, slot):
@@ -269,11 +309,13 @@ def tile_shiftedpatchtokenization_pb_t_kernel(tc, x, ln2_g, ln2_b, w2, b2, tok, 
                 nc.sync.dma_start(out=out_v[:, :, r, :], in_=ot[:])
 
             load(0)
+            load(1)
             for slot in range(10):
                 norm(0, slot)
+            add_bias(0)
             for r in range(16):
-                if r + 1 < 16:
-                    load(r + 1)
+                if r + 2 < 16:
+                    load(r + 2)
                 zc_t = cpool.tile([P, 5, 256], U32, name="zc", align_bytes=64)
                 zs_t = cpool.tile([P, 5, 256], U8, name="zs", align_bytes=64)
                 codes[r] = (zc_t, zs_t)
@@ -303,6 +345,8 @@ def tile_shiftedpatchtokenization_pb_t_kernel(tc, x, ln2_g, ln2_b, w2, b2, tok, 
                     if g5 >= 1:
                         quantise(r, g5 - 1)
                 quantise(r, 4)
+                if r + 1 < 16:
+                    add_bias(r + 1)
                 if r >= 1:
                     project(r - 1)
             project(15)

@@ -55,12 +55,14 @@ def tile_shiftedpatchtokenization_pb_t_kernel(tc, x, ln2_g, ln2_b, w2, b2, tok, 
         one = keep.tile([P, 1], F32)
         mask_top = keep.tile([P, 1], F32)
         mask_bot = keep.tile([P, 1], F32)
+        neg_id = keep.tile([P, P], BF16)
 
         nc.vector.memset(one[:], 1.0)
         nc.scalar.sqrt(one[:], one[:])
 
         make_identity(nc, ident[:])
         id8 = ident[:].rearrange("p (a b) -> p a b", b=8)
+        nc.vector.tensor_scalar(out=neg_id[:], in0=ident[:], scalar1=-1.0, scalar2=None, op0=ALU.mult)
         nc.vector.memset(sh_dn[:], 0.0)
         nc.vector.memset(sh_up[:], 0.0)
         nc.vector.tensor_copy(out=sh_dn[:, 1:P], in_=ident[:, 0 : P - 1])
@@ -115,23 +117,33 @@ def tile_shiftedpatchtokenization_pb_t_kernel(tc, x, ln2_g, ln2_b, w2, b2, tok, 
                     op0=ALU.mult, op1=ALU.subtract,
                 )
                 nc.vector.tensor_tensor(out=h[:], in0=h[:], in1=xq[:, :, :, 1, :, 0], op=ALU.subtract)
-                nc.vector.tensor_tensor(out=h[:], in0=h[:], in1=xq[:, :, :, 1, :, 1], op=ALU.subtract)
                 hs[i] = h
 
-            def relayout(i):
-                u = ORDER[i]
+            def turn_first(i):
                 h = hs[i]
+                xq = xss[i][:].rearrange("p g (o e x f) -> p g o e x f", o=2, e=2, x=128, f=2)
                 m_t = m_a if i % 2 == 0 else m_b
                 m_v = m_t[:, 4:2052].rearrange("p (c o b g) -> p c o b g", c=8, o=2, b=16)
                 for o in range(2):
                     for hq in range(2):
                         p1 = psa.tile([P, 4, P], F32, name="p1")
                         for gq in range(4):
-                            nc.tensor.transpose(p1[:, gq, :], h[:, 4 * hq + gq, o, :], ident[:])
+                            nc.tensor.matmul(
+                                out=p1[:, gq, :], lhsT=h[:, 4 * hq + gq, o, :], rhs=ident[:],
+                                is_transpose=True, start=True, stop=False,
+                            )
+                            nc.tensor.matmul(
+                                out=p1[:, gq, :], lhsT=xq[:, 4 * hq + gq, o, 1, :, 1], rhs=neg_id[:],
+                                start=False, stop=True,
+                            )
                         nc.scalar.copy(
                             out=m_v[:, :, o, :, 4 * hq : 4 * hq + 4],
                             in_=p1[:].rearrange("p q (b c) -> p c b q", c=8),
                         )
+
+            def turn_second(i):
+                u = ORDER[i]
+                m_t = m_a if i % 2 == 0 else m_b
                 for o in range(2):
                     ro = 2 * u + o
                     jobs = [(4 + ro, 0, None)]
@@ -166,10 +178,11 @@ def tile_shiftedpatchtokenization_pb_t_kernel(tc, x, ln2_g, ln2_b, w2, b2, tok, 
                 )
                 nc.vector.tensor_copy(out=CR[:, :, 1 + q, 1:33], in_=CS[:, :, q, :])
 
-            for i in range(3):
-                load_chunk(i)
+            load_chunk(0)
+            load_chunk(1)
             nc.sync.dma_start(out=g0b[0:20, :], in_=ln2_g.rearrange("(s p) -> s p", p=P))
             nc.sync.dma_start(out=g0b[32:52, :], in_=ln2_b.rearrange("(s p) -> s p", p=P))
+            load_chunk(2)
             nc.sync.dma_start(out=b2bc[:], in_=b2.partition_broadcast(P))
 
             def load_w(g5):
@@ -179,17 +192,17 @@ def tile_shiftedpatchtokenization_pb_t_kernel(tc, x, ln2_g, ln2_b, w2, b2, tok, 
             load_w(0)
             load_w(1)
 
-            for i in range(10):
+            for i in range(11):
                 if i < 8:
                     haar(i)
                     if i + 3 < 8:
                         load_chunk(i + 3)
-                if i == 0:
+                if i == 2:
                     nc.vector.tensor_copy(out=g0f[:], in_=g0b[:])
                     gps = psx.tile([P, P], F32, name="gps", tag="misc")
                     nc.tensor.transpose(gps[:], g0f[:], ident[:])
                     nc.vector.tensor_copy(out=gb[:], in_=gps[:])
-                if i == 6:
+                if i == 7:
                     cs_flat = CS[:].rearrange("p k q x -> p (k q x)")
                     pdn = psx.tile([P, 2, 4, 32], F32, name="pdn", tag="misc")
                     pup = psx.tile([P, 2, 4, 32], F32, name="pup", tag="misc")
@@ -198,7 +211,9 @@ def tile_shiftedpatchtokenization_pb_t_kernel(tc, x, ln2_g, ln2_b, w2, b2, tok, 
                     nc.vector.tensor_copy(out=CR[:, :, 0, 1:33], in_=pdn[:, :, 3, :])
                     nc.vector.tensor_copy(out=CR[:, :, 5, 1:33], in_=pup[:, :, 0, :])
                 if 1 <= i <= 8:
-                    relayout(i - 1)
+                    turn_first(i - 1)
+                if 2 <= i <= 9:
+                    turn_second(i - 2)
                 if 1 <= i <= 5:
                     wgrps[i - 1] = wpool.tile([P, DIM, 4], BF16, name="wgrp", align_bytes=64)
                     nc.scalar.copy(out=wgrps[i - 1][:], in_=wraws[i - 1][:].rearrange("p t n -> p n t"))
@@ -210,8 +225,8 @@ def tile_shiftedpatchtokenization_pb_t_kernel(tc, x, ln2_g, ln2_b, w2, b2, tok, 
                         scales=ws[:, i - 2, :],
                         in_=wgrps[i - 2][:].rearrange("p n t -> p (n t)"),
                     )
-                if i >= 3 and i % 2 == 1:
-                    cell_sums(ORDER[i - 3] // 2)
+                if i >= 4 and i % 2 == 0:
+                    cell_sums(ORDER[i - 4] // 2)
 
             nc.vector.tensor_tensor(out=A1[:], in0=CR[:, :, 0:5, :], in1=CR[:, :, 1:6, :], op=ALU.add)
             nc.vector.tensor_tensor(out=Rw[:], in0=A1[:, :, 0:3:2, :], in1=A1[:, :, 2:5:2, :], op=ALU.add)

@@ -130,11 +130,12 @@ def tile_shiftedpatchtokenization_pb_t_kernel(tc, x, ln2_g, ln2_b, w2, b2, tok, 
                         for gq in range(4):
                             nc.tensor.matmul(
                                 out=p1[:, gq, :], lhsT=h[:, 4 * hq + gq, o, :], rhs=ident[:],
-                                is_transpose=True, start=True, stop=False,
+                                is_transpose=True, start=(gq == 0), stop=False,
                             )
+                        for gq in range(4):
                             nc.tensor.matmul(
                                 out=p1[:, gq, :], lhsT=xq[:, 4 * hq + gq, o, 1, :, 1], rhs=neg_id[:],
-                                start=False, stop=True,
+                                start=False, stop=(gq == 3),
                             )
                         nc.scalar.copy(
                             out=m_v[:, :, o, :, 4 * hq : 4 * hq + 4],

from contextlib import ExitStack

import concourse.mybir as mybir
from concourse.masks import make_identity

F32 = mybir.dt.float32
BF16 = mybir.dt.bfloat16
U32 = mybir.dt.uint32
U8 = mybir.dt.uint8
FP8X4 = mybir.dt.float8_e4m3fn_x4
ALU = mybir.AluOpType
ACT = mybir.ActivationFunctionType
AX = mybir.AxisListType

P = 128
KDIM = 2560
DIM = 512
FLOPS = 2 * 4096 * KDIM * DIM

ROW0 = (4, 0, 0, 8, 8)
COL0 = (4, 0, 8, 0, 8)
S_SLOTS = (1, 5, 9)
ORDER = (6, 7, 0, 1, 2, 3, 4, 5)


def tile_shiftedpatchtokenization_pb_t_kernel(tc, x, ln2_g, ln2_b, w2, b2, tok, out):
    nc = tc.nc
    xv = x.rearrange("b c (g u r) w -> (b c) g u (r w)", g=8, u=8)
    wv = w2.rearrange("(g t p) n -> g p t n", t=4, p=P)
    tok_v = tok.rearrange("b (g e j) d -> (b g) e j d", g=8, e=2)
    out_v = out.rearrange("b (g e j) d -> (b g) e j d", g=8, e=2)

    with ExitStack() as ctx:
        keep = ctx.enter_context(tc.tile_pool(name="keep", bufs=1))
        ident = keep.tile([P, P], F32)
        sh_dn = keep.tile([P, P], F32)
        sh_up = keep.tile([P, P], F32)
        gb = keep.tile([P, P], F32)
        b2bc = keep.tile([P, DIM], BF16)
        wc = keep.tile([P, 5, DIM], U32, align_bytes=64)
        ws = keep.tile([P, 5, DIM], U8, align_bytes=64)
        W = keep.tile([P, 24, 136, 8], F32)
        CS = keep.tile([P, 2, 4, 32], F32)
        CR = keep.tile([P, 2, 6, 34], F32)
        A1 = keep.tile([P, 2, 5, 34], F32)
        Rw = keep.tile([P, 2, 2, 34], F32)
        Bw = keep.tile([P, 2, 2, 33], F32)
        Bc = keep.tile([P, 2, 2, 33], F32)
        ST = keep.tile([P, 2, 2, 16], F32)
        mean = keep.tile([P, 32], F32)
        va = keep.tile([P, 32], F32)
        tmp = keep.tile([P, 32], F32)
        rstd = keep.tile([P, 32], F32)
        nbias = keep.tile([P, 32], F32)
        one = keep.tile([P, 1], F32)
        mask_top = keep.tile([P, 1], F32)
        mask_bot = keep.tile([P, 1], F32)
        neg_id = keep.tile([P, P], BF16)

        nc.vector.memset(one[:], 1.0)
        nc.scalar.sqrt(one[:], one[:])

        make_identity(nc, ident[:])
        id8 = ident[:].rearrange("p (a b) -> p a b", b=8)
        nc.vector.tensor_scalar(out=neg_id[:], in0=ident[:], scalar1=-1.0, scalar2=None, op0=ALU.mult)
        nc.vector.memset(sh_dn[:], 0.0)
        nc.vector.memset(sh_up[:], 0.0)
        nc.vector.tensor_copy(out=sh_dn[:, 1:P], in_=ident[:, 0 : P - 1])
        nc.vector.tensor_copy(out=sh_up[:, 0 : P - 1], in_=ident[:, 1:P])
        nc.vector.memset(sh_dn[:].rearrange("p (a b) -> p a b", b=8)[:, :, 0:1], 0.0)
        nc.vector.memset(sh_up[:].rearrange("p (a b) -> p a b", b=8)[:, :, 7:8], 0.0)
        nc.vector.tensor_reduce(out=mask_top[:], in_=id8[:, :, 0], axis=AX.X, op=ALU.add)
        nc.vector.tensor_reduce(out=mask_bot[:], in_=id8[:, :, 7], axis=AX.X, op=ALU.add)
        nc.vector.tensor_scalar(out=mask_top[:], in0=mask_top[:], scalar1=-1.0, scalar2=1.0, op0=ALU.mult, op1=ALU.add)
        nc.vector.tensor_scalar(out=mask_bot[:], in0=mask_bot[:], scalar1=-1.0, scalar2=1.0, op0=ALU.mult, op1=ALU.add)
        nc.vector.memset(W[:, :, 0:4, :], 0.0)
        nc.vector.memset(W[:, :, 132:136, :], 0.0)
        nc.vector.memset(CR[:], 0.0)
        nc.vector.memset(CS[:], 0.0)

        with ExitStack() as pa:
            xpool = pa.enter_context(tc.tile_pool(name="xpool", bufs=3))
            hpool = pa.enter_context(tc.tile_pool(name="hpool", bufs=2))
            tpool = pa.enter_context(tc.tile_pool(name="tpool", bufs=1))
            psa = pa.enter_context(tc.psum_pool(name="psa", bufs=3))
            psx = pa.enter_context(tc.psum_pool(name="psx", bufs=2))

            m_a = tpool.tile([P, 2056], F32)
            m_b = tpool.tile([P, 2056], F32)
            for m_t in (m_a, m_b):
                nc.vector.memset(m_t[:, 0:4], 0.0)
                nc.vector.memset(m_t[:, 2052:2056], 0.0)
            g0b = tpool.tile([P, P], BF16)
            g0f = tpool.tile([P, P], F32)
            nc.vector.memset(g0b[:], 0.0)
            bns = tpool.tile([P, 4, 32, 6], F32)
            sq_a = tpool.tile([P, 32], F32)
            sq_b = tpool.tile([P, 32], F32)
            wpool = pa.enter_context(tc.tile_pool(name="wpool", bufs=2))
            wraws = {}
            wgrps = {}

            pa.enter_context(tc.manual_schedule())
            xss = {}
            hs = {}

            def load_chunk(i):
                xs = xpool.tile([P, 8, 1024], BF16, name="xs")
                nc.sync.dma_start(out=xs[:], in_=xv[:, :, ORDER[i], :])
                xss[i] = xs

            def haar(i):
                xq = xss[i][:].rearrange("p g (o e x f) -> p g o e x f", o=2, e=2, x=128, f=2)
                h = hpool.tile([P, 8, 2, 128], F32, name="h")
                nc.vector.scalar_tensor_tensor(
                    out=h[:], in0=xq[:, :, :, 0, :, 0], scalar=3.0, in1=xq[:, :, :, 0, :, 1],
                    op0=ALU.mult, op1=ALU.subtract,
                )
                nc.vector.tensor_tensor(out=h[:], in0=h[:], in1=xq[:, :, :, 1, :, 0], op=ALU.subtract)
                hs[i] = h

            def turn_first(i):
                h = hs[i]
                xq = xss[i][:].rearrange("p g (o e x f) -> p g o e x f", o=2, e=2, x=128, f=2)
                m_t = m_a if i % 2 == 0 else m_b
                m_v = m_t[:, 4:2052].rearrange("p (c o b g) -> p c o b g", c=8, o=2, b=16)
                for o in range(2):
                    for hq in range(2):
                        p1 = psa.tile([P, 4, P], F32, name="p1")
                        for gq in range(4):
                            nc.tensor.matmul(
                                out=p1[:, gq, :], lhsT=h[:, 4 * hq + gq, o, :], rhs=ident[:],
                                is_transpose=True, start=(gq == 0), stop=False,
                            )
                        for gq in range(4):
                            nc.tensor.matmul(
                                out=p1[:, gq, :], lhsT=xq[:, 4 * hq + gq, o, 1, :, 1], rhs=neg_id[:],
                                start=False, stop=(gq == 3),
                            )
                        nc.scalar.copy(
                            out=m_v[:, :, o, :, 4 * hq : 4 * hq + 4],
                            in_=p1[:].rearrange("p q (b c) -> p c b q", c=8),
                        )

            def turn_second(i):
                u = ORDER[i]
                m_t = m_a if i % 2 == 0 else m_b
                for o in range(2):
                    ro = 2 * u + o
                    jobs = [(4 + ro, 0, None)]
                    if ro < 4:
                        jobs.append((20 + ro, 1, mask_bot))
                    if ro >= 12:
                        jobs.append((ro - 12, -1, mask_top))
                    for r, shift, mask in jobs:
                        for ch in range(2):
                            p2 = psa.tile([P, 4, P], F32, name="p2")
                            for c4 in range(4):
                                base = 4 + ((4 * ch + c4) * 2 + o) * P + shift
                                nc.tensor.transpose(p2[:, c4, :], m_t[:, base : base + P], ident[:])
                            dst = W[:, r, 4:132, 4 * ch : 4 * ch + 4]
                            srcv = p2[:].rearrange("p c x -> p x c")
                            if mask is None:
                                nc.scalar.copy(out=dst, in_=srcv)
                            else:
                                nc.scalar.activation(out=dst, in_=srcv, func=ACT.Copy, scale=mask[:, 0:1])

            def cell_sums(q):
                r0 = 4 + 4 * q
                for cx in range(32):
                    nc.vector.bn_stats(out=bns[:, q, cx, :], in_=W[:, r0 : r0 + 4, 4 + 4 * cx : 8 + 4 * cx, :])
                nc.vector.tensor_tensor(out=CS[:, 0, q, :], in0=bns[:, q, :, 1], in1=bns[:, q, :, 4], op=ALU.add)
                nc.vector.tensor_tensor(out=sq_a[:], in0=bns[:, q, :, 1], in1=bns[:, q, :, 1], op=ALU.mult)
                nc.vector.tensor_tensor(out=sq_b[:], in0=bns[:, q, :, 4], in1=bns[:, q, :, 4], op=ALU.mult)
                nc.vector.tensor_tensor(out=sq_a[:], in0=sq_a[:], in1=sq_b[:], op=ALU.add)
                nc.vector.tensor_tensor(out=sq_b[:], in0=bns[:, q, :, 2], in1=bns[:, q, :, 5], op=ALU.add)
                nc.vector.scalar_tensor_tensor(
                    out=CS[:, 1, q, :], in0=sq_a[:], scalar=64.0, in1=sq_b[:], op0=ALU.mult, op1=ALU.add
                )
                nc.vector.tensor_copy(out=CR[:, :, 1 + q, 1:33], in_=CS[:, :, q, :])

            load_chunk(0)
            load_chunk(1)
            nc.sync.dma_start(out=g0b[0:20, :], in_=ln2_g.rearrange("(s p) -> s p", p=P))
            nc.sync.dma_start(out=g0b[32:52, :], in_=ln2_b.rearrange("(s p) -> s p", p=P))
            load_chunk(2)
            nc.sync.dma_start(out=b2bc[:], in_=b2.partition_broadcast(P))

            def load_w(g5):
                wraws[g5] = wpool.tile([P, 4, DIM], BF16, name="wraw")
                nc.sync.dma_start(out=wraws[g5][:], in_=wv[g5])

            load_w(0)
            load_w(1)

            for i in range(11):
                if i < 8:
                    haar(i)
                    if i + 3 < 8:
                        load_chunk(i + 3)
                if i == 2:
                    nc.vector.tensor_copy(out=g0f[:], in_=g0b[:])
                    gps = psx.tile([P, P], F32, name="gps", tag="misc")
                    nc.tensor.transpose(gps[:], g0f[:], ident[:])
                    nc.vector.tensor_copy(out=gb[:], in_=gps[:])
                if i == 7:
                    cs_flat = CS[:].rearrange("p k q x -> p (k q x)")
                    pdn = psx.tile([P, 2, 4, 32], F32, name="pdn", tag="misc")
                    pup = psx.tile([P, 2, 4, 32], F32, name="pup", tag="misc")
                    nc.tensor.matmul(out=pdn[:].rearrange("p k q x -> p (k q x)"), lhsT=sh_dn[:], rhs=cs_flat, start=True, stop=True)
                    nc.tensor.matmul(out=pup[:].rearrange("p k q x -> p (k q x)"), lhsT=sh_up[:], rhs=cs_flat, start=True, stop=True)
                    nc.vector.tensor_copy(out=CR[:, :, 0, 1:33], in_=pdn[:, :, 3, :])
                    nc.vector.tensor_copy(out=CR[:, :, 5, 1:33], in_=pup[:, :, 0, :])
                if 1 <= i <= 8:
                    turn_first(i - 1)
                if 2 <= i <= 9:
                    turn_second(i - 2)
                if 1 <= i <= 5:
                    wgrps[i - 1] = wpool.tile([P, DIM, 4], BF16, name="wgrp", align_bytes=64)
                    nc.scalar.copy(out=wgrps[i - 1][:], in_=wraws[i - 1][:].rearrange("p t n -> p n t"))
                    if i + 1 < 5:
                        load_w(i + 1)
                if 2 <= i <= 6:
                    nc.vector.quantize_mx(
                        out=wc[:, i - 2, :].bitcast(FP8X4),
                        scales=ws[:, i - 2, :],
                        in_=wgrps[i - 2][:].rearrange("p n t -> p (n t)"),
                    )
                if i >= 4 and i % 2 == 0:
                    cell_sums(ORDER[i - 4] // 2)

            nc.vector.tensor_tensor(out=A1[:], in0=CR[:, :, 0:5, :], in1=CR[:, :, 1:6, :], op=ALU.add)
            nc.vector.tensor_tensor(out=Rw[:], in0=A1[:, :, 0:3:2, :], in1=A1[:, :, 2:5:2, :], op=ALU.add)
            nc.vector.tensor_tensor(out=Bw[:], in0=Rw[:, :, :, 0:33], in1=Rw[:, :, :, 1:34], op=ALU.add)
            nc.vector.tensor_tensor(out=Bc[:], in0=A1[:, :, 1:4:2, 0:33], in1=A1[:, :, 1:4:2, 1:34], op=ALU.add)
            nc.vector.tensor_tensor(out=ST[:], in0=Bw[:, :, :, 0:31:2], in1=Bw[:, :, :, 2:33:2], op=ALU.add)
            nc.vector.tensor_tensor(out=ST[:], in0=ST[:], in1=Bc[:, :, :, 1:32:2], op=ALU.add)
            s1 = ST[:, 0, :, :].rearrange("p e j -> p (e j)")
            s2 = ST[:, 1, :, :].rearrange("p e j -> p (e j)")
            nc.vector.tensor_scalar(out=mean[:], in0=s1, scalar1=64.0 / KDIM, scalar2=None, op0=ALU.mult)
            nc.vector.tensor_tensor(out=tmp[:], in0=mean[:], in1=mean[:], op=ALU.mult)
            nc.vector.tensor_scalar(out=va[:], in0=s2, scalar1=1.0 / KDIM, scalar2=36.0e-5, op0=ALU.mult, op1=ALU.add)
            nc.vector.tensor_tensor(out=va[:], in0=va[:], in1=tmp[:], op=ALU.subtract)
            nc.scalar.sqrt(tmp[:], va[:])
            nc.vector.reciprocal(rstd[:], tmp[:])
            nc.vector.tensor_tensor(out=tmp[:], in0=rstd[:], in1=rstd[:], op=ALU.mult)
            nc.vector.tensor_tensor(out=tmp[:], in0=tmp[:], in1=va[:], op=ALU.mult)
            nc.vector.tensor_scalar(out=tmp[:], in0=tmp[:], scalar1=-0.5, scalar2=1.5, op0=ALU.mult, op1=ALU.add)
            nc.vector.tensor_tensor(out=rstd[:], in0=rstd[:], in1=tmp[:], op=ALU.mult)
            nc.vector.scalar_tensor_tensor(
                out=nbias[:], in0=mean[:], scalar=-1.0, in1=rstd[:], op0=ALU.mult, op1=ALU.mult
            )

        with ExitStack() as pb:
            npool = pb.enter_context(tc.tile_pool(name="npool", bufs=4))
            zpool = pb.enter_context(tc.tile_pool(name="zpool", bufs=3))
            cpool = pb.enter_context(tc.tile_pool(name="cpool", bufs=2))
            iopool = pb.enter_context(tc.tile_pool(name="iopool", bufs=3))
            pst = pb.enter_context(tc.psum_pool(name="pst", bufs=6))
            psm = pb.enter_context(tc.psum_pool(name="psm", bufs=2))
            pb.enter_context(tc.manual_schedule())

            nbs = {}
            tbs = {}
            tks = {}
            codes = {}
            zis = {}

            def load(r):
                tks[r] = iopool.tile([P, 2, DIM], BF16, name="tk")
                nc.sync.dma_start(out=tks[r][:], in_=tok_v[:, :, r, :])

            def add_bias(r):
                tb = iopool.tile([P, 2, DIM], F32, name="tb")
                nc.vector.tensor_tensor(
                    out=tb[:], in0=tks[r][:], in1=b2bc[:].unsqueeze(1).to_broadcast([P, 2, DIM]), op=ALU.add
                )
                tbs[r] = tb

            def norm(r, slot):
                e, s = divmod(slot, 5)
                if s == 0:
                    nbs[(r, e)] = npool.tile([P, KDIM], F32, name="nb")
                nbv = nbs[(r, e)][:].rearrange("p (a b s c) -> p a b s c", a=8, b=8, s=5)
                col = 16 * e + r
                srcw = W[:, 8 * e + ROW0[s] : 8 * e + ROW0[s] + 8, 8 * r + COL0[s] : 8 * r + COL0[s] + 8, :]
                if slot in S_SLOTS:
                    nc.scalar.activation(
                        out=nbv[:, :, :, s, :], in_=srcw, func=ACT.Identity,
                        scale=rstd[:, col : col + 1], bias=nbias[:, col : col + 1],
                    )
                else:
                    nc.vector.tensor_scalar(
                        out=nbv[:, :, :, s, :], in0=srcw,
                        scalar1=rstd[:, col : col + 1], scalar2=nbias[:, col : col + 1],
                        op0=ALU.mult, op1=ALU.add,
                    )

            def quantise(r, g5):
                zc, zs = codes[r]
                nc.vector.quantize_mx(
                    out=zc[:, g5, :].bitcast(FP8X4), scales=zs[:, g5, :],
                    in_=zis[(r, g5)][:].rearrange("p c t -> p (c t)"),
                )

            def project(r):
                zc, zs = codes[r]
                ot = iopool.tile([P, 2, DIM], F32, name="ot")
                accs = []
                for u in range(2):
                    acc = psm.tile([P, DIM], F32, name="acc")
                    for g5 in range(5):
                        nc.tensor.matmul_mx(
                            out=acc[:],
                            lhsT=zc[:, g5, P * u : P * u + P].bitcast(FP8X4),
                            lhsT_scale=zs[:, g5, P * u : P * u + P],
                            rhs=wc[:, g5, :].bitcast(FP8X4),
                            rhs_scale=ws[:, g5, :],
                            start=(g5 == 0),
                            stop=(g5 == 4),
                        )
                    accs.append(acc)
                for u in range(2):
                    nc.vector.tensor_tensor(out=ot[:, u, :], in0=accs[u][:], in1=tbs[r][:, u, :], op=ALU.add)
                nc.sync.dma_start(out=out_v[:, :, r, :], in_=ot[:])

            load(0)
            load(1)
            for slot in range(10):
                norm(0, slot)
            add_bias(0)
            for r in range(16):
                if r + 2 < 16:
                    load(r + 2)
                zc_t = cpool.tile([P, 5, 256], U32, name="zc", align_bytes=64)
                zs_t = cpool.tile([P, 5, 256], U8, name="zs", align_bytes=64)
                codes[r] = (zc_t, zs_t)
                for g5 in range(5):
                    zp = zpool.tile([P, 4, 256], BF16, name="zp")
                    for half in range(2):
                        pt = pst.tile([P, 2, 2, P], F32, name="pt")
                        for a in range(2):
                            sl = 4 * g5 + 2 * half + a
                            for u in range(2):
                                nc.tensor.transpose(pt[:, a, u, :], nbs[(r, u)][:, P * sl : P * sl + P], ident[:])
                        for a in range(2):
                            sl = 4 * g5 + 2 * half + a
                            nc.scalar.activation(
                                out=zp[:, 2 * half + a, :], in_=pt[:, a, :, :].rearrange("p u r -> p (u r)"),
                                func=ACT.Identity, scale=gb[:, sl : sl + 1], bias=gb[:, 32 + sl : 33 + sl],
                            )
                    if r + 1 < 16:
                        norm(r + 1, 2 * g5)
                        norm(r + 1, 2 * g5 + 1)
                    zi = zpool.tile([P, 256, 4], BF16, name="zi", align_bytes=64)
                    zis[(r, g5)] = zi
                    nc.vector.tensor_copy(
                        out=zi[:].rearrange("p (c i) t -> p c t i", i=4),
                        in_=zp[:].rearrange("p t (c i) -> p c t i", i=4),
                    )
                    if g5 >= 1:
                        quantise(r, g5 - 1)
                quantise(r, 4)
                if r + 1 < 16:
                    add_bias(r + 1)
                if r >= 1:
                    project(r - 1)
            project(15)
